import numpy as np
import ml_dtypes


def mxq(x, axis, fmt="e4m3"):
    dtype, down = {"e4m3": (ml_dtypes.float8_e4m3fn, 7), "e5m2": (ml_dtypes.float8_e5m2, 14)}[fmt]
    v = np.moveaxis(np.asarray(x, np.float32).astype(ml_dtypes.bfloat16).astype(np.float64), axis, -1)
    blocks = v.reshape(v.shape[:-1] + (-1, 32))
    amax = np.abs(blocks).max(-1, keepdims=True)
    byte = np.maximum(np.where(amax > 0, np.frexp(amax)[1] - 1 + 127, 0) - down, 1)
    scale = np.exp2(byte - 127.0)
    codes = (blocks / scale).astype(np.float32).astype(dtype).astype(np.float64)
    return np.moveaxis((codes * scale).reshape(v.shape), -1, axis)


WIDE = False


def mx_kscale(k):
    if not WIDE:
        return np.ones(k)
    levels = np.array([10, -10, 5, -5, 0])
    a = np.random.permutation(np.resize(levels, k // 512 * 4)).reshape(k // 512, 4)
    idx = np.arange(k)
    return np.exp2(a[idx // 512, idx % 128 // 32])


BF16 = ml_dtypes.bfloat16


def bf(x):
    return np.asarray(x, np.float32).astype(BF16)


def f64(x):
    return np.asarray(x).astype(np.float64)


NUM_PLANES = 80
BOARD = 8 * 8
IN_DIM = NUM_PLANES * BOARD
OUT_DIM = 1920
B = 512


def setup_inputs():
    s = mx_kscale(IN_DIM)
    x = np.random.standard_normal((B, NUM_PLANES, 8, 8)) * s.reshape(NUM_PLANES, 8, 8)
    rows = np.random.randint(0, IN_DIM, size=OUT_DIM)
    m = np.random.standard_normal((IN_DIM, OUT_DIM)) * 0.01
    m[rows, np.arange(OUT_DIM)] += 1.0
    return {"x": bf(x), "fc1": bf(m / s[:, None])}


def reference(x, fc1):
    h = f64(x).reshape(-1, IN_DIM)
    return mxq(h, 1, "e4m3") @ mxq(f64(fc1), 0, "e4m3")

@@ -1,0 +1,208 @@
+from contextlib import ExitStack
+
+import concourse.mybir as mybir
+from concourse.masks import make_identity
+
+FLOPS = 2 * 512 * 5120 * 1920
+
+BF16 = mybir.dt.bfloat16
+F32 = mybir.dt.float32
+U32 = mybir.dt.uint32
+U8 = mybir.dt.uint8
+FP8X4 = mybir.dt.float8_e4m3fn_x4
+
+P = 128
+K = 5120
+K_PASS = 512
+PASSES = K // K_PASS
+M_TILES = 4
+WIN = 512
+ROUNDS = ((0, 1024), (1024, 896))
+RAW_BUFS = 8
+
+
+def tile_applypolicymap_kernel(tc, x, fc1, out):
+    nc = tc.nc
+    h = x.rearrange("b c r s -> b (c r s)")
+    chunks = [(r, g) for r in range(2) for g in range(PASSES)]
+    n_chunks = len(chunks)
+
+    with ExitStack() as ctx:
+        const = ctx.enter_context(tc.tile_pool(name="const", bufs=1))
+        xraw_pool = ctx.enter_context(tc.tile_pool(name="xraw", bufs=4))
+        xgrp_pool = ctx.enter_context(tc.tile_pool(name="xgrp", bufs=2))
+        raw_pool = ctx.enter_context(tc.tile_pool(name="raw", bufs=RAW_BUFS))
+        grp_pool = ctx.enter_context(tc.tile_pool(name="grp", bufs=3))
+        code_pool = ctx.enter_context(tc.tile_pool(name="code", bufs=4))
+        oa_pool = ctx.enter_context(tc.tile_pool(name="oa", bufs=4))
+        ob_pool = ctx.enter_context(tc.tile_pool(name="ob", bufs=8))
+        psum = ctx.enter_context(tc.psum_pool(name="psum", bufs=1))
+
+        ident = const.tile([P, P], F32, name="ident")
+        make_identity(nc, ident[:])
+        x_codes = [const.tile([P, PASSES * P], U32, name="xc%d" % m, align_bytes=64) for m in range(M_TILES)]
+        x_scales = [const.tile([P, PASSES * P], U8, name="xs%d" % m, align_bytes=64) for m in range(M_TILES)]
+
+        ctx.enter_context(tc.manual_schedule())
+
+        x_raw = []
+        for m in range(M_TILES):
+            xr = xraw_pool.tile([P, K], BF16, name="xr%d" % m, tag="xr")
+            rows = h[m * P : (m + 1) * P, :]
+            nc.sync.dma_start(out=xr[:, 0:2048], in_=rows[:, 0:2048])
+            nc.sync.dma_start(out=xr[:, 2048:K], in_=rows[:, 2048:K])
+            x_raw.append(xr)
+
+        raw = {}
+
+        def load(i):
+            r, g = chunks[i]
+            c0, w = ROUNDS[r]
+            t = raw_pool.tile([P, 4, w], BF16, name="raw%d" % i, tag="raw")
+            for u in range(2):
+                k0 = K_PASS * g + 256 * u
+                nc.sync.dma_start(
+                    out=t[:, 2 * u : 2 * u + 2, :],
+                    in_=fc1[k0 : k0 + 256, c0 : c0 + w].rearrange("(p e) w -> p e w", e=2),
+                )
+            raw[i] = t
+
+        for i in range(RAW_BUFS):
+            load(i)
+
+        x_grp = {}
+
+        def quantise_x(m, g0, g1):
+            nc.vector.quantize_mx(
+                out=x_codes[m][:, g0 * P : g1 * P].bitcast(FP8X4),
+                scales=x_scales[m][:, g0 * P : g1 * P],
+                in_=x_grp[m][:, g0 * 4 * P : g1 * 4 * P],
+            )
+
+        for m in range(M_TILES):
+            words = x_raw[m][:].bitcast(F32)
+            xg = xgrp_pool.tile([P, K], BF16, name="xg%d" % m, tag="xg", align_bytes=64)
+            x_grp[m] = xg
+            xg_words = xg[:].bitcast(F32)
+            banks = []
+            for j in range(5):
+                b = 5 * m + j
+                xt = psum.tile([P, WIN], F32, name="xt%d" % b, tag="bank%d" % (b % 8))
+                for q in range(4):
+                    w0 = WIN * j + P * q
+                    nc.tensor.transpose(xt[:, q * P : (q + 1) * P], words[:, w0 : w0 + P], ident[:])
+                banks.append(xt)
+            for j in (0, 2, 3, 4, 1):
+                dst = xg_words[:, WIN * j : WIN * (j + 1)].rearrange("p (g b u) -> p g b u", g=2, b=P, u=2)
+                src = banks[j][:].rearrange("p (g u b) -> p g b u", g=2, u=2, b=P)
+                if j == 1:
+                    nc.vector.tensor_copy(out=dst, in_=src)
+                else:
+                    nc.scalar.copy(out=dst, in_=src)
+            if m > 0:
+                quantise_x(m - 1, 8, 10)
+            quantise_x(m, 0, 4)
+            quantise_x(m, 4, 8)
+        quantise_x(M_TILES - 1, 8, 10)
+
+        grp_v = {}
+        grp_s = {}
+        codes = {}
+        scales = {}
+        acc = {}
+        o_a = {}
+
+        def regroup(i):
+            r, g = chunks[i]
+            w = ROUNDS[r][1]
+            gv = grp_pool.tile([P, 4 * WIN], BF16, name="gv%d" % i, tag="gv", align_bytes=64)
+            gs = grp_pool.tile([P, 4 * WIN], BF16, name="gs%d" % i, tag="gs", align_bytes=64)
+            nc.vector.tensor_copy(
+                out=gv[:].rearrange("p (c i t) -> p c t i", i=4, t=4),
+                in_=raw[i][:, :, 0:WIN].rearrange("p t (c i) -> p c t i", i=4),
+            )
+            nc.scalar.copy(
+                out=gs[:, 0 : 4 * (w - WIN)].rearrange("p (c i t) -> p c t i", i=4, t=4),
+                in_=raw[i][:, :, WIN:w].rearrange("p t (c i) -> p c t i", i=4),
+            )
+            grp_v[i] = gv
+            grp_s[i] = gs
+
+        def quantise_v(i):
+            codes[i] = code_pool.tile([P, 1024], U32, name="cd%d" % i, tag="cd", align_bytes=64)
+            scales[i] = code_pool.tile([P, 1024], U8, name="sc%d" % i, tag="sc", align_bytes=64)
+            nc.vector.quantize_mx(
+                out=codes[i][:, 0:WIN].bitcast(FP8X4), scales=scales[i][:, 0:WIN], in_=grp_v[i][:]
+            )
+
+        def quantise_s(i):
+            w = ROUNDS[chunks[i][0]][1]
+            c = WIN
+            for n in (512, 256, 128):
+                if w - c >= n:
+                    nc.vector.quantize_mx(
+                        out=codes[i][:, c : c + n].bitcast(FP8X4),
+                        scales=scales[i][:, c : c + n],
+                        in_=grp_s[i][:, 4 * (c - WIN) : 4 * (c - WIN + n)],
+                    )
+                    c += n
+
+        def passes(i, hw):
+            r, g = chunks[i]
+            w = ROUNDS[r][1]
+            w0 = 0 if hw == 0 else w - WIN
+            for m in range(M_TILES):
+                if g == 0:
+                    acc[(r, m, hw)] = psum.tile(
+                        [P, WIN], F32, name="acc%d_%d_%d" % (r, m, hw), tag="bank%d" % (2 * m + hw)
+                    )
+                nc.tensor.matmul_mx(
+                    out=acc[(r, m, hw)][:],
+                    lhsT=x_codes[m][:, g * P : (g + 1) * P].bitcast(FP8X4),
+                    lhsT_scale=x_scales[m][:, g * P : (g + 1) * P],
+                    rhs=codes[i][:, w0 : w0 + WIN].bitcast(FP8X4),
+                    rhs_scale=scales[i][:, w0 : w0 + WIN],
+                    start=(g == 0),
+                    stop=(g == PASSES - 1),
+                )
+
+        def copy_out(engine, dst, src):
+            if engine == "S":
+                nc.scalar.copy(out=dst, in_=src)
+            else:
+                nc.vector.tensor_copy(out=dst, in_=src)
+
+        def evac_a(hw, engines):
+            for m in range(M_TILES):
+                if hw == 0:
+                    o_a[m] = oa_pool.tile([P, 1024], F32, name="oa%d" % m, tag="oa")
+                copy_out(engines[m], o_a[m][:, hw * WIN : (hw + 1) * WIN], acc[(0, m, hw)][:])
+
+        for i in range(n_chunks):
+            regroup(i)
+            if i + RAW_BUFS < n_chunks:
+                load(i + RAW_BUFS)
+            if i == PASSES:
+                evac_a(0, "SVSV")
+            if i == PASSES + 1:
+                evac_a(1, "SSSS")
+                for m in range(M_TILES):
+                    nc.sync.dma_start(out=out[m * P : (m + 1) * P, 0:1024], in_=o_a[m][:])
+            if i >= 1:
+                quantise_s(i - 1)
+                passes(i - 1, 1)
+            quantise_v(i)
+            passes(i, 0)
+        quantise_s(n_chunks - 1)
+        passes(n_chunks - 1, 1)
+
+        c0, w = ROUNDS[1]
+        k = 0
+        for hw in range(2):
+            for m in range(M_TILES):
+                n = WIN if hw == 0 else w - WIN
+                ob = ob_pool.tile([P, WIN], F32, name="ob%d_%d" % (m, hw), tag="ob")
+                copy_out("SV"[k % 2], ob[:, 0:n], acc[(1, m, hw)][:, WIN - n : WIN])
+                k += 1
+                col = c0 + hw * WIN
+                nc.sync.dma_start(out=out[m * P : (m + 1) * P, col : col + n], in_=ob[:, 0:n])

@@ -19,6 +19,7 @@ M_TILES = 4
 WIN = 512
 ROUNDS = ((0, 1024), (1024, 896))
 RAW_BUFS = 8
+V_COLS = (512, 448)
 
 
 def tile_applypolicymap_kernel(tc, x, fc1, out):
@@ -117,10 +118,16 @@ def tile_applypolicymap_kernel(tc, x, fc1, out):
             w = ROUNDS[r][1]
             gv = grp_pool.tile([P, 4 * WIN], BF16, name="gv%d" % i, tag="gv", align_bytes=64)
             gs = grp_pool.tile([P, 4 * WIN], BF16, name="gs%d" % i, tag="gs", align_bytes=64)
+            nv = V_COLS[r]
             nc.vector.tensor_copy(
-                out=gv[:].rearrange("p (c i t) -> p c t i", i=4, t=4),
-                in_=raw[i][:, :, 0:WIN].rearrange("p t (c i) -> p c t i", i=4),
+                out=gv[:, 0 : 4 * nv].rearrange("p (c i t) -> p c t i", i=4, t=4),
+                in_=raw[i][:, :, 0:nv].rearrange("p t (c i) -> p c t i", i=4),
             )
+            if nv < WIN:
+                nc.scalar.copy(
+                    out=gv[:, 4 * nv : 4 * WIN].rearrange("p (c i t) -> p c t i", i=4, t=4),
+                    in_=raw[i][:, :, nv:WIN].rearrange("p t (c i) -> p c t i", i=4),
+                )
             nc.scalar.copy(
                 out=gs[:, 0 : 4 * (w - WIN)].rearrange("p (c i t) -> p c t i", i=4, t=4),
                 in_=raw[i][:, :, WIN:w].rearrange("p t (c i) -> p c t i", i=4),
@@ -150,21 +157,27 @@ def tile_applypolicymap_kernel(tc, x, fc1, out):
         def passes(i, hw):
             r, g = chunks[i]
             w = ROUNDS[r][1]
-            w0 = 0 if hw == 0 else w - WIN
+            if hw == 0:
+                parts = [(0, WIN)]
+            elif w - WIN == WIN:
+                parts = [(WIN, WIN)]
+            else:
+                parts = [(WIN, 256), (WIN + 256, 128)]
             for m in range(M_TILES):
                 if g == 0:
                     acc[(r, m, hw)] = psum.tile(
                         [P, WIN], F32, name="acc%d_%d_%d" % (r, m, hw), tag="bank%d" % (2 * m + hw)
                     )
-                nc.tensor.matmul_mx(
-                    out=acc[(r, m, hw)][:],
-                    lhsT=x_codes[m][:, g * P : (g + 1) * P].bitcast(FP8X4),
-                    lhsT_scale=x_scales[m][:, g * P : (g + 1) * P],
-                    rhs=codes[i][:, w0 : w0 + WIN].bitcast(FP8X4),
-                    rhs_scale=scales[i][:, w0 : w0 + WIN],
-                    start=(g == 0),
-                    stop=(g == PASSES - 1),
-                )
+                for k, (c, n) in enumerate(parts):
+                    nc.tensor.matmul_mx(
+                        out=acc[(r, m, hw)][:, c - hw * WIN : c - hw * WIN + n],
+                        lhsT=x_codes[m][:, g * P : (g + 1) * P].bitcast(FP8X4),
+                        lhsT_scale=x_scales[m][:, g * P : (g + 1) * P],
+                        rhs=codes[i][:, c : c + n].bitcast(FP8X4),
+                        rhs_scale=scales[i][:, c : c + n],
+                        start=(g == 0 and k == 0),
+                        stop=(g == PASSES - 1 and k == len(parts) - 1),
+                    )
 
         def copy_out(engine, dst, src):
             if engine == "S":
@@ -183,7 +196,7 @@ def tile_applypolicymap_kernel(tc, x, fc1, out):
             if i + RAW_BUFS < n_chunks:
                 load(i + RAW_BUFS)
             if i == PASSES:
-                evac_a(0, "SVSV")
+                evac_a(0, "VVVS")
             if i == PASSES + 1:
                 evac_a(1, "SSSS")
                 for m in range(M_TILES):
@@ -202,7 +215,7 @@ def tile_applypolicymap_kernel(tc, x, fc1, out):
             for m in range(M_TILES):
                 n = WIN if hw == 0 else w - WIN
                 ob = ob_pool.tile([P, WIN], F32, name="ob%d_%d" % (m, hw), tag="ob")
-                copy_out("SV"[k % 2], ob[:, 0:n], acc[(1, m, hw)][:, WIN - n : WIN])
+                copy_out("SV"[k % 2], ob[:, 0:n], acc[(1, m, hw)][:, 0:n])
                 k += 1
                 col = c0 + hw * WIN
                 nc.sync.dma_start(out=out[m * P : (m + 1) * P, col : col + n], in_=ob[:, 0:n])

@@ -20,6 +20,9 @@ WIN = 512
 ROUNDS = ((0, 1024), (1024, 896))
 RAW_BUFS = 8
 V_COLS = (512, 448)
+TAIL = 2
+TAIL_V = (320, 224)
+TAIL_OUT = ("SSSV", "SVSV")
 
 
 def tile_applypolicymap_kernel(tc, x, fc1, out):
@@ -113,27 +116,21 @@ def tile_applypolicymap_kernel(tc, x, fc1, out):
         acc = {}
         o_a = {}
 
-        def regroup(i):
-            r, g = chunks[i]
-            w = ROUNDS[r][1]
-            gv = grp_pool.tile([P, 4 * WIN], BF16, name="gv%d" % i, tag="gv", align_bytes=64)
-            gs = grp_pool.tile([P, 4 * WIN], BF16, name="gs%d" % i, tag="gs", align_bytes=64)
-            nv = V_COLS[r]
-            nc.vector.tensor_copy(
-                out=gv[:, 0 : 4 * nv].rearrange("p (c i t) -> p c t i", i=4, t=4),
-                in_=raw[i][:, :, 0:nv].rearrange("p t (c i) -> p c t i", i=4),
-            )
-            if nv < WIN:
-                nc.scalar.copy(
-                    out=gv[:, 4 * nv : 4 * WIN].rearrange("p (c i t) -> p c t i", i=4, t=4),
-                    in_=raw[i][:, :, nv:WIN].rearrange("p t (c i) -> p c t i", i=4),
-                )
-            nc.scalar.copy(
-                out=gs[:, 0 : 4 * (w - WIN)].rearrange("p (c i t) -> p c t i", i=4, t=4),
-                in_=raw[i][:, :, WIN:w].rearrange("p t (c i) -> p c t i", i=4),
-            )
-            grp_v[i] = gv
-            grp_s[i] = gs
+        def regroup_cols(i, dst, lo, hi, split):
+            for mover, c0, c1 in ((nc.vector.tensor_copy, lo, split), (nc.scalar.copy, split, hi)):
+                if c1 > c0:
+                    mover(
+                        out=dst[:, 4 * (c0 - lo) : 4 * (c1 - lo)].rearrange("p (c i t) -> p c t i", i=4, t=4),
+                        in_=raw[i][:, :, c0:c1].rearrange("p t (c i) -> p c t i", i=4),
+                    )
+
+        def regroup_first(i, split):
+            grp_v[i] = grp_pool.tile([P, 4 * WIN], BF16, name="gv%d" % i, tag="gv", align_bytes=64)
+            regroup_cols(i, grp_v[i], 0, WIN, split)
+
+        def regroup_second(i, split):
+            grp_s[i] = grp_pool.tile([P, 4 * WIN], BF16, name="gs%d" % i, tag="gs", align_bytes=64)
+            regroup_cols(i, grp_s[i], WIN, ROUNDS[chunks[i][0]][1], split)
 
         def quantise_v(i):
             codes[i] = code_pool.tile([P, 1024], U32, name="cd%d" % i, tag="cd", align_bytes=64)
@@ -191,8 +188,9 @@ def tile_applypolicymap_kernel(tc, x, fc1, out):
                     o_a[m] = oa_pool.tile([P, 1024], F32, name="oa%d" % m, tag="oa")
                 copy_out(engines[m], o_a[m][:, hw * WIN : (hw + 1) * WIN], acc[(0, m, hw)][:])
 
-        for i in range(n_chunks):
-            regroup(i)
+        for i in range(n_chunks - TAIL):
+            regroup_first(i, V_COLS[chunks[i][0]])
+            regroup_second(i, WIN)
             if i + RAW_BUFS < n_chunks:
                 load(i + RAW_BUFS)
             if i == PASSES:
@@ -206,16 +204,29 @@ def tile_applypolicymap_kernel(tc, x, fc1, out):
                 passes(i - 1, 1)
             quantise_v(i)
             passes(i, 0)
-        quantise_s(n_chunks - 1)
-        passes(n_chunks - 1, 1)
+
+        t0 = n_chunks - TAIL
+        regroup_first(t0, TAIL_V[0])
+        quantise_s(t0 - 1)
+        passes(t0 - 1, 1)
+        for i in range(t0 + 1, n_chunks):
+            regroup_first(i, TAIL_V[0])
+            quantise_v(i - 1)
+            passes(i - 1, 0)
+        regroup_second(t0, WIN + TAIL_V[1])
+        quantise_v(n_chunks - 1)
+        passes(n_chunks - 1, 0)
+        for i in range(t0 + 1, n_chunks):
+            regroup_second(i, WIN + TAIL_V[1])
+        for i in range(t0, n_chunks):
+            quantise_s(i)
+            passes(i, 1)
 
         c0, w = ROUNDS[1]
-        k = 0
         for hw in range(2):
             for m in range(M_TILES):
                 n = WIN if hw == 0 else w - WIN
                 ob = ob_pool.tile([P, WIN], F32, name="ob%d_%d" % (m, hw), tag="ob")
-                copy_out("SV"[k % 2], ob[:, 0:n], acc[(1, m, hw)][:, 0:n])
-                k += 1
+                copy_out(TAIL_OUT[hw][m], ob[:, 0:n], acc[(1, m, hw)][:, 0:n])
                 col = c0 + hw * WIN
                 nc.sync.dma_start(out=out[m * P : (m + 1) * P, col : col + n], in_=ob[:, 0:n])

@@ -19,7 +19,7 @@ M_TILES = 4
 WIN = 512
 ROUNDS = ((0, 1024), (1024, 896))
 RAW_BUFS = 8
-V_COLS = (512, 448)
+V_COLS = (512, 480)
 TAIL = 2
 TAIL_V = (320, 224)
 TAIL_OUT = ("SSSV", "SVSV")

from contextlib import ExitStack

import concourse.mybir as mybir
from concourse.masks import make_identity

FLOPS = 2 * 512 * 5120 * 1920

BF16 = mybir.dt.bfloat16
F32 = mybir.dt.float32
U32 = mybir.dt.uint32
U8 = mybir.dt.uint8
FP8X4 = mybir.dt.float8_e4m3fn_x4

P = 128
K = 5120
K_PASS = 512
PASSES = K // K_PASS
M_TILES = 4
WIN = 512
ROUNDS = ((0, 1024), (1024, 896))
RAW_BUFS = 8
V_COLS = (512, 480)
TAIL = 2
TAIL_V = (320, 224)
TAIL_OUT = ("SSSV", "SVSV")


def tile_applypolicymap_kernel(tc, x, fc1, out):
    nc = tc.nc
    h = x.rearrange("b c r s -> b (c r s)")
    chunks = [(r, g) for r in range(2) for g in range(PASSES)]
    n_chunks = len(chunks)

    with ExitStack() as ctx:
        const = ctx.enter_context(tc.tile_pool(name="const", bufs=1))
        xraw_pool = ctx.enter_context(tc.tile_pool(name="xraw", bufs=4))
        xgrp_pool = ctx.enter_context(tc.tile_pool(name="xgrp", bufs=2))
        raw_pool = ctx.enter_context(tc.tile_pool(name="raw", bufs=RAW_BUFS))
        grp_pool = ctx.enter_context(tc.tile_pool(name="grp", bufs=3))
        code_pool = ctx.enter_context(tc.tile_pool(name="code", bufs=4))
        oa_pool = ctx.enter_context(tc.tile_pool(name="oa", bufs=4))
        ob_pool = ctx.enter_context(tc.tile_pool(name="ob", bufs=8))
        psum = ctx.enter_context(tc.psum_pool(name="psum", bufs=1))

        ident = const.tile([P, P], F32, name="ident")
        make_identity(nc, ident[:])
        x_codes = [const.tile([P, PASSES * P], U32, name="xc%d" % m, align_bytes=64) for m in range(M_TILES)]
        x_scales = [const.tile([P, PASSES * P], U8, name="xs%d" % m, align_bytes=64) for m in range(M_TILES)]

        ctx.enter_context(tc.manual_schedule())

        x_raw = []
        for m in range(M_TILES):
            xr = xraw_pool.tile([P, K], BF16, name="xr%d" % m, tag="xr")
            rows = h[m * P : (m + 1) * P, :]
            nc.sync.dma_start(out=xr[:, 0:2048], in_=rows[:, 0:2048])
            nc.sync.dma_start(out=xr[:, 2048:K], in_=rows[:, 2048:K])
            x_raw.append(xr)

        raw = {}

        def load(i):
            r, g = chunks[i]
            c0, w = ROUNDS[r]
            t = raw_pool.tile([P, 4, w], BF16, name="raw%d" % i, tag="raw")
            for u in range(2):
                k0 = K_PASS * g + 256 * u
                nc.sync.dma_start(
                    out=t[:, 2 * u : 2 * u + 2, :],
                    in_=fc1[k0 : k0 + 256, c0 : c0 + w].rearrange("(p e) w -> p e w", e=2),
                )
            raw[i] = t

        for i in range(RAW_BUFS):
            load(i)

        x_grp = {}

        def quantise_x(m, g0, g1):
            nc.vector.quantize_mx(
                out=x_codes[m][:, g0 * P : g1 * P].bitcast(FP8X4),
                scales=x_scales[m][:, g0 * P : g1 * P],
                in_=x_grp[m][:, g0 * 4 * P : g1 * 4 * P],
            )

        for m in range(M_TILES):
            words = x_raw[m][:].bitcast(F32)
            xg = xgrp_pool.tile([P, K], BF16, name="xg%d" % m, tag="xg", align_bytes=64)
            x_grp[m] = xg
            xg_words = xg[:].bitcast(F32)
            banks = []
            for j in range(5):
                b = 5 * m + j
                xt = psum.tile([P, WIN], F32, name="xt%d" % b, tag="bank%d" % (b % 8))
                for q in range(4):
                    w0 = WIN * j + P * q
                    nc.tensor.transpose(xt[:, q * P : (q + 1) * P], words[:, w0 : w0 + P], ident[:])
                banks.append(xt)
            for j in (0, 2, 3, 4, 1):
                dst = xg_words[:, WIN * j : WIN * (j + 1)].rearrange("p (g b u) -> p g b u", g=2, b=P, u=2)
                src = banks[j][:].rearrange("p (g u b) -> p g b u", g=2, u=2, b=P)
                if j == 1:
                    nc.vector.tensor_copy(out=dst, in_=src)
                else:
                    nc.scalar.copy(out=dst, in_=src)
            if m > 0:
                quantise_x(m - 1, 8, 10)
            quantise_x(m, 0, 4)
            quantise_x(m, 4, 8)
        quantise_x(M_TILES - 1, 8, 10)

        grp_v = {}
        grp_s = {}
        codes = {}
        scales = {}
        acc = {}
        o_a = {}

        def regroup_cols(i, dst, lo, hi, split):
            for mover, c0, c1 in ((nc.vector.tensor_copy, lo, split), (nc.scalar.copy, split, hi)):
                if c1 > c0:
                    mover(
                        out=dst[:, 4 * (c0 - lo) : 4 * (c1 - lo)].rearrange("p (c i t) -> p c t i", i=4, t=4),
                        in_=raw[i][:, :, c0:c1].rearrange("p t (c i) -> p c t i", i=4),
                    )

        def regroup_first(i, split):
            grp_v[i] = grp_pool.tile([P, 4 * WIN], BF16, name="gv%d" % i, tag="gv", align_bytes=64)
            regroup_cols(i, grp_v[i], 0, WIN, split)

        def regroup_second(i, split):
            grp_s[i] = grp_pool.tile([P, 4 * WIN], BF16, name="gs%d" % i, tag="gs", align_bytes=64)
            regroup_cols(i, grp_s[i], WIN, ROUNDS[chunks[i][0]][1], split)

        def quantise_v(i):
            codes[i] = code_pool.tile([P, 1024], U32, name="cd%d" % i, tag="cd", align_bytes=64)
            scales[i] = code_pool.tile([P, 1024], U8, name="sc%d" % i, tag="sc", align_bytes=64)
            nc.vector.quantize_mx(
                out=codes[i][:, 0:WIN].bitcast(FP8X4), scales=scales[i][:, 0:WIN], in_=grp_v[i][:]
            )

        def quantise_s(i):
            w = ROUNDS[chunks[i][0]][1]
            c = WIN
            for n in (512, 256, 128):
                if w - c >= n:
                    nc.vector.quantize_mx(
                        out=codes[i][:, c : c + n].bitcast(FP8X4),
                        scales=scales[i][:, c : c + n],
                        in_=grp_s[i][:, 4 * (c - WIN) : 4 * (c - WIN + n)],
                    )
                    c += n

        def passes(i, hw):
            r, g = chunks[i]
            w = ROUNDS[r][1]
            if hw == 0:
                parts = [(0, WIN)]
            elif w - WIN == WIN:
                parts = [(WIN, WIN)]
            else:
                parts = [(WIN, 256), (WIN + 256, 128)]
            for m in range(M_TILES):
                if g == 0:
                    acc[(r, m, hw)] = psum.tile(
                        [P, WIN], F32, name="acc%d_%d_%d" % (r, m, hw), tag="bank%d" % (2 * m + hw)
                    )
                for k, (c, n) in enumerate(parts):
                    nc.tensor.matmul_mx(
                        out=acc[(r, m, hw)][:, c - hw * WIN : c - hw * WIN + n],
                        lhsT=x_codes[m][:, g * P : (g + 1) * P].bitcast(FP8X4),
                        lhsT_scale=x_scales[m][:, g * P : (g + 1) * P],
                        rhs=codes[i][:, c : c + n].bitcast(FP8X4),
                        rhs_scale=scales[i][:, c : c + n],
                        start=(g == 0 and k == 0),
                        stop=(g == PASSES - 1 and k == len(parts) - 1),
                    )

        def copy_out(engine, dst, src):
            if engine == "S":
                nc.scalar.copy(out=dst, in_=src)
            else:
                nc.vector.tensor_copy(out=dst, in_=src)

        def evac_a(hw, engines):
            for m in range(M_TILES):
                if hw == 0:
                    o_a[m] = oa_pool.tile([P, 1024], F32, name="oa%d" % m, tag="oa")
                copy_out(engines[m], o_a[m][:, hw * WIN : (hw + 1) * WIN], acc[(0, m, hw)][:])

        for i in range(n_chunks - TAIL):
            regroup_first(i, V_COLS[chunks[i][0]])
            regroup_second(i, WIN)
            if i + RAW_BUFS < n_chunks:
                load(i + RAW_BUFS)
            if i == PASSES:
                evac_a(0, "VVVS")
            if i == PASSES + 1:
                evac_a(1, "SSSS")
                for m in range(M_TILES):
                    nc.sync.dma_start(out=out[m * P : (m + 1) * P, 0:1024], in_=o_a[m][:])
            if i >= 1:
                quantise_s(i - 1)
                passes(i - 1, 1)
            quantise_v(i)
            passes(i, 0)

        t0 = n_chunks - TAIL
        regroup_first(t0, TAIL_V[0])
        quantise_s(t0 - 1)
        passes(t0 - 1, 1)
        for i in range(t0 + 1, n_chunks):
            regroup_first(i, TAIL_V[0])
            quantise_v(i - 1)
            passes(i - 1, 0)
        regroup_second(t0, WIN + TAIL_V[1])
        quantise_v(n_chunks - 1)
        passes(n_chunks - 1, 0)
        for i in range(t0 + 1, n_chunks):
            regroup_second(i, WIN + TAIL_V[1])
        for i in range(t0, n_chunks):
            quantise_s(i)
            passes(i, 1)

        c0, w = ROUNDS[1]
        for hw in range(2):
            for m in range(M_TILES):
                n = WIN if hw == 0 else w - WIN
                ob = ob_pool.tile([P, WIN], F32, name="ob%d_%d" % (m, hw), tag="ob")
                copy_out(TAIL_OUT[hw][m], ob[:, 0:n], acc[(1, m, hw)][:, 0:n])
                col = c0 + hw * WIN
                nc.sync.dma_start(out=out[m * P : (m + 1) * P, col : col + n], in_=ob[:, 0:n])
